import numpy as np
import ml_dtypes


def mxq(x, axis, fmt="e4m3"):
    dtype, down = {"e4m3": (ml_dtypes.float8_e4m3fn, 7), "e5m2": (ml_dtypes.float8_e5m2, 14)}[fmt]
    v = np.moveaxis(np.asarray(x, np.float32).astype(ml_dtypes.bfloat16).astype(np.float64), axis, -1)
    blocks = v.reshape(v.shape[:-1] + (-1, 32))
    amax = np.abs(blocks).max(-1, keepdims=True)
    byte = np.maximum(np.where(amax > 0, np.frexp(amax)[1] - 1 + 127, 0) - down, 1)
    scale = np.exp2(byte - 127.0)
    codes = (blocks / scale).astype(np.float32).astype(dtype).astype(np.float64)
    return np.moveaxis((codes * scale).reshape(v.shape), -1, axis)


WIDE = False


def mx_kscale(k):
    if not WIDE:
        return np.ones(k)
    levels = np.array([10, -10, 5, -5, 0])
    a = np.random.permutation(np.resize(levels, k // 512 * 4)).reshape(k // 512, 4)
    idx = np.arange(k)
    return np.exp2(a[idx // 512, idx % 128 // 32])


BF16 = ml_dtypes.bfloat16


def bf(x):
    return np.asarray(x, np.float32).astype(BF16)


def f64(x):
    return np.asarray(x).astype(np.float64)


B, S, D, DM, DK = 2, 512, 1024, 1024, 64
LN_EPS = 1e-5


def setup_inputs():
    s = mx_kscale(DM)
    return {
        "h_attn": bf(np.random.standard_normal((B, S, DM)) * 0.3 * s),
        "Wo": bf(np.random.standard_normal((DM, D)) * 3.0 / np.sqrt(DM) / s[:, None]),
        "bo": bf(np.random.standard_normal((B, S, D)) * 0.5 + np.random.uniform(0.25, 0.75, (B, 1, 1))),
        "x": bf(np.random.standard_normal((B, S, D))),
        "gamma": bf(1.0 + 0.1 * np.random.standard_normal((S, D))),
        "beta": bf(0.1 * np.random.standard_normal((S, D))),
    }


def reference(h_attn, Wo, bo, x, gamma, beta):
    o = (mxq(f64(h_attn), 2, "e4m3") @ mxq(f64(Wo), 0, "e4m3")) + f64(bo)
    o = o + f64(x)
    mu = o.mean(axis=(-2, -1), keepdims=True)
    var = np.square(o - mu).mean(axis=(-2, -1), keepdims=True)
    return (o - mu) / np.sqrt(var + LN_EPS) * f64(gamma) + f64(beta)

@@ -1,0 +1,273 @@
+from contextlib import ExitStack
+
+import concourse.mybir as mybir
+from concourse.masks import make_identity
+
+F32 = mybir.dt.float32
+BF16 = mybir.dt.bfloat16
+U32 = mybir.dt.uint32
+U8 = mybir.dt.uint8
+FP8X4 = mybir.dt.float8_e4m3fn_x4
+ALU = mybir.AluOpType
+ACT = mybir.ActivationFunctionType
+AXIS = mybir.AxisListType
+
+P = 128
+BATCH = 2
+SEQ = 512
+K = 1024
+N = 1024
+LN_EPS = 1e-5
+
+PACK = 4
+K_PASS = P * PACK
+PASSES = K // K_PASS
+HALVES = 2
+N_BLOCK = 512
+N_BLOCKS = N // N_BLOCK
+TILES = SEQ // P
+RUN = 4
+
+VECTOR_COLS = 672
+
+FLOPS = 2 * BATCH * SEQ * K * N
+
+
+def tile_multiheadattn_pb_kernel(tc, h_attn, Wo, bo, x, gamma, beta, out):
+    nc = tc.nc
+    with ExitStack() as ctx:
+        const = ctx.enter_context(tc.tile_pool(name="const", bufs=1))
+        keep = ctx.enter_context(tc.tile_pool(name="keep", bufs=1))
+        scratch = ctx.enter_context(tc.tile_pool(name="scratch", bufs=4))
+        psum_t = ctx.enter_context(tc.psum_pool(name="psum_t", bufs=2))
+        psum_acc = ctx.enter_context(tc.psum_pool(name="psum_acc", bufs=4))
+        psum_stat = ctx.enter_context(tc.psum_pool(name="psum_stat", bufs=2))
+
+        ident = const.tile([P, P], F32)
+        make_identity(nc, ident[:])
+        mean_w = const.tile([P, P], F32)
+        nc.vector.memset(mean_w[:], 1.0 / (SEQ * N))
+        eps = const.tile([P, 1], F32)
+        nc.vector.memset(eps[:], LN_EPS)
+        warm = const.tile([P, 1], F32)
+        nc.scalar.activation(out=warm[:], in_=eps[:], func=ACT.Sqrt)
+
+        h_view = h_attn.rearrange("b (p j) k -> b p j k", j=TILES)
+        bo_view = bo.rearrange("b (p j) n -> b p j n", j=TILES)
+        x_view = x.rearrange("b (p j) n -> b p j n", j=TILES)
+        gamma_view = gamma.rearrange("(p j) n -> p j n", j=TILES)
+        beta_view = beta.rearrange("(p j) n -> p j n", j=TILES)
+        out_view = out.rearrange("b (p j) n -> b p j n", j=TILES)
+
+        def load_in_halves(dst, src):
+            half = TILES // 2
+            for first in (0, half):
+                nc.sync.dma_start(
+                    out=dst[:, first : first + half, :], in_=src[:, first : first + half, :]
+                )
+
+        wo_raw = []
+        for g in range(PASSES):
+            raw = keep.tile([P, PACK, N], BF16, name="wo_raw%d" % g)
+            for u in range(HALVES):
+                first = K_PASS * g + (K_PASS // HALVES) * u
+                nc.sync.dma_start(
+                    out=raw[:, 2 * u : 2 * u + 2, :],
+                    in_=Wo[first : first + K_PASS // HALVES, :].rearrange(
+                        "(q e) c -> q e c", e=2
+                    ),
+                )
+            wo_raw.append(raw)
+
+        h_raw = [keep.tile([P, TILES, K], BF16, name="h_raw%d" % b) for b in range(BATCH)]
+        bo_sb = [keep.tile([P, TILES, N], BF16, name="bo_sb%d" % b) for b in range(BATCH)]
+        x_sb = [keep.tile([P, TILES, N], BF16, name="x_sb%d" % b) for b in range(BATCH)]
+        gamma_sb = keep.tile([P, TILES, N], BF16)
+        beta_sb = keep.tile([P, TILES, N], BF16)
+
+        def load_bias_and_residual(b):
+            half = TILES // 2
+            for first in (0, half):
+                tiles = slice(first, first + half)
+                nc.sync.dma_start(out=bo_sb[b][:, tiles, :], in_=bo_view[b, :, tiles, :])
+                nc.sync.dma_start(out=x_sb[b][:, tiles, :], in_=x_view[b, :, tiles, :])
+
+        load_in_halves(h_raw[0], h_view[0])
+        load_bias_and_residual(0)
+        load_bias_and_residual(1)
+        load_in_halves(h_raw[1], h_view[1])
+        load_in_halves(gamma_sb, gamma_view)
+        load_in_halves(beta_sb, beta_view)
+
+        wo_codes = []
+        wo_scales = []
+        for g in range(PASSES):
+            grouped = keep.tile([P, N, PACK], BF16, name="wo_grouped%d" % g, align_bytes=64)
+            for copy, cols in (
+                (nc.vector.tensor_copy, slice(0, VECTOR_COLS)),
+                (nc.scalar.copy, slice(VECTOR_COLS, N)),
+            ):
+                copy(
+                    out=grouped[:, cols, :].rearrange("p (c i) t -> p c t i", i=RUN),
+                    in_=wo_raw[g][:, :, cols].rearrange("p t (c i) -> p c t i", i=RUN),
+                )
+            codes = keep.tile([P, N], U32, name="wo_codes%d" % g, align_bytes=64)
+            scales = keep.tile([P, N], U8, name="wo_scales%d" % g, align_bytes=64)
+            for n in range(N_BLOCKS):
+                cols = slice(N_BLOCK * n, N_BLOCK * (n + 1))
+                nc.vector.quantize_mx(
+                    out=codes[:, cols].bitcast(FP8X4),
+                    scales=scales[:, cols],
+                    in_=grouped[:, cols, :].rearrange("p c t -> p (c t)"),
+                )
+            wo_codes.append(codes)
+            wo_scales.append(scales)
+
+        o_sb = [
+            [keep.tile([P, N], F32, name="o_sb%d_%d" % (b, j)) for j in range(TILES)]
+            for b in range(BATCH)
+        ]
+        h_codes = [
+            [
+                keep.tile([P, PASSES * P], U32, name="h_codes%d_%d" % (b, j), align_bytes=64)
+                for j in range(TILES)
+            ]
+            for b in range(BATCH)
+        ]
+        h_scales = [
+            [
+                keep.tile([P, PASSES * P], U8, name="h_scales%d_%d" % (b, j), align_bytes=64)
+                for j in range(TILES)
+            ]
+            for b in range(BATCH)
+        ]
+        chunk_sums = [
+            keep.tile([P, TILES * N_BLOCKS], F32, name="chunk_sums%d" % b) for b in range(BATCH)
+        ]
+        square_sums = [keep.tile([P, TILES], F32, name="square_sums%d" % b) for b in range(BATCH)]
+        neg_mean = [keep.tile([P, 1], F32, name="neg_mean%d" % b) for b in range(BATCH)]
+        rstd = [keep.tile([P, 1], F32, name="rstd%d" % b) for b in range(BATCH)]
+
+        def quantise_h(b):
+            for j in range(TILES):
+                words = h_raw[b][:, j, :].bitcast(F32)
+                turned = psum_t.tile([P, PASSES, HALVES, P], F32, name="turned")
+                for g in range(PASSES):
+                    for u in range(HALVES):
+                        first = P * (HALVES * g + u)
+                        nc.tensor.transpose(
+                            turned[:, g, u, :], words[:, first : first + P], ident[:]
+                        )
+                grouped = keep.tile(
+                    [P, PASSES, P, PACK], BF16, name="h_grouped%d_%d" % (b, j), align_bytes=64
+                )
+                nc.scalar.copy(
+                    out=grouped[:].bitcast(F32),
+                    in_=turned[:].rearrange("p g u r -> p g r u"),
+                )
+                nc.vector.quantize_mx(
+                    out=h_codes[b][j][:].bitcast(FP8X4),
+                    scales=h_scales[b][j][:],
+                    in_=grouped[:].rearrange("p g r t -> p (g r t)"),
+                )
+
+        def add_bias_and_residual(engine, b):
+            for j in range(TILES):
+                engine.tensor_tensor(
+                    out=o_sb[b][j][:], in0=bo_sb[b][:, j, :], in1=x_sb[b][:, j, :], op=ALU.add
+                )
+
+        def project(b):
+            for j in range(TILES):
+                for n in range(N_BLOCKS):
+                    cols = slice(N_BLOCK * n, N_BLOCK * (n + 1))
+                    acc = psum_acc.tile([P, N_BLOCK], F32, name="acc")
+                    for g in range(PASSES):
+                        tokens = slice(P * g, P * (g + 1))
+                        nc.tensor.matmul_mx(
+                            out=acc[:],
+                            lhsT=h_codes[b][j][:, tokens].bitcast(FP8X4),
+                            lhsT_scale=h_scales[b][j][:, tokens],
+                            rhs=wo_codes[g][:, cols].bitcast(FP8X4),
+                            rhs_scale=wo_scales[g][:, cols],
+                            start=(g == 0),
+                            stop=(g == PASSES - 1),
+                        )
+                    chunk = N_BLOCKS * j + n
+                    nc.vector.scalar_tensor_tensor(
+                        out=o_sb[b][j][:, cols],
+                        in0=acc[:],
+                        scalar=1.0,
+                        in1=o_sb[b][j][:, cols],
+                        op0=ALU.mult,
+                        op1=ALU.add,
+                        accum_out=chunk_sums[b][:, chunk : chunk + 1],
+                    )
+
+        def mean_over_all(sums):
+            row = scratch.tile([P, 1], F32, name="row")
+            nc.vector.reduce_sum(out=row[:], in_=sums[:], axis=AXIS.X)
+            mean = psum_stat.tile([P, 1], F32, name="mean")
+            nc.tensor.matmul(out=mean[:], lhsT=mean_w[:], rhs=row[:], start=True, stop=True)
+            return mean
+
+        def find_mean(b):
+            mean = mean_over_all(chunk_sums[b])
+            nc.vector.tensor_scalar_mul(out=neg_mean[b][:], in0=mean[:], scalar1=-1.0)
+
+        def find_rstd(b):
+            for j in range(TILES):
+                squares = scratch.tile([P, N], BF16, name="squares")
+                nc.scalar.activation(
+                    out=squares[:],
+                    in_=o_sb[b][j][:],
+                    func=ACT.Square,
+                    bias=neg_mean[b][:],
+                    scale=1.0,
+                    accum_out=square_sums[b][:, j : j + 1],
+                )
+            var = mean_over_all(square_sums[b])
+            std = scratch.tile([P, 1], F32, name="std")
+            nc.scalar.activation(out=std[:], in_=var[:], func=ACT.Sqrt, bias=eps[:], scale=1.0)
+            nc.vector.reciprocal(out=rstd[b][:], in_=std[:])
+
+        def centre_and_gain(b, j):
+            nc.vector.scalar_tensor_tensor(
+                out=o_sb[b][j][:],
+                in0=o_sb[b][j][:],
+                scalar=neg_mean[b][:],
+                in1=gamma_sb[:, j, :],
+                op0=ALU.add,
+                op1=ALU.mult,
+            )
+
+        def scale_shift_store(b, j):
+            nc.vector.scalar_tensor_tensor(
+                out=o_sb[b][j][:],
+                in0=o_sb[b][j][:],
+                scalar=rstd[b][:],
+                in1=beta_sb[:, j, :],
+                op0=ALU.mult,
+                op1=ALU.add,
+            )
+            nc.sync.dma_start(out=out_view[b, :, j, :], in_=o_sb[b][j][:])
+
+        def normalise(b):
+            centre_and_gain(b, 0)
+            for j in range(1, TILES):
+                centre_and_gain(b, j)
+                scale_shift_store(b, j - 1)
+            scale_shift_store(b, TILES - 1)
+
+        quantise_h(0)
+        add_bias_and_residual(nc.vector, 0)
+        add_bias_and_residual(nc.gpsimd, 1)
+        project(0)
+        find_mean(0)
+        quantise_h(1)
+        project(1)
+        find_rstd(0)
+        find_mean(1)
+        normalise(0)
+        find_rstd(1)
+        normalise(1)

@@ -10,7 +10,6 @@ U8 = mybir.dt.uint8
 FP8X4 = mybir.dt.float8_e4m3fn_x4
 ALU = mybir.AluOpType
 ACT = mybir.ActivationFunctionType
-AXIS = mybir.AxisListType
 
 P = 128
 BATCH = 2
@@ -42,6 +41,7 @@ def tile_multiheadattn_pb_kernel(tc, h_attn, Wo, bo, x, gamma, beta, out):
         psum_t = ctx.enter_context(tc.psum_pool(name="psum_t", bufs=2))
         psum_acc = ctx.enter_context(tc.psum_pool(name="psum_acc", bufs=4))
         psum_stat = ctx.enter_context(tc.psum_pool(name="psum_stat", bufs=2))
+        ctx.enter_context(tc.manual_schedule())
 
         ident = const.tile([P, P], F32)
         make_identity(nc, ident[:])
@@ -93,14 +93,13 @@ def tile_multiheadattn_pb_kernel(tc, h_attn, Wo, bo, x, gamma, beta, out):
                 nc.sync.dma_start(out=x_sb[b][:, tiles, :], in_=x_view[b, :, tiles, :])
 
         load_in_halves(h_raw[0], h_view[0])
+        load_in_halves(h_raw[1], h_view[1])
         load_bias_and_residual(0)
         load_bias_and_residual(1)
-        load_in_halves(h_raw[1], h_view[1])
         load_in_halves(gamma_sb, gamma_view)
         load_in_halves(beta_sb, beta_view)
 
-        wo_codes = []
-        wo_scales = []
+        wo_grouped = []
         for g in range(PASSES):
             grouped = keep.tile([P, N, PACK], BF16, name="wo_grouped%d" % g, align_bytes=64)
             for copy, cols in (
@@ -111,17 +110,21 @@ def tile_multiheadattn_pb_kernel(tc, h_attn, Wo, bo, x, gamma, beta, out):
                     out=grouped[:, cols, :].rearrange("p (c i) t -> p c t i", i=RUN),
                     in_=wo_raw[g][:, :, cols].rearrange("p t (c i) -> p c t i", i=RUN),
                 )
-            codes = keep.tile([P, N], U32, name="wo_codes%d" % g, align_bytes=64)
-            scales = keep.tile([P, N], U8, name="wo_scales%d" % g, align_bytes=64)
-            for n in range(N_BLOCKS):
-                cols = slice(N_BLOCK * n, N_BLOCK * (n + 1))
+            wo_grouped.append(grouped)
+        wo_codes = [
+            keep.tile([P, N], U32, name="wo_codes%d" % g, align_bytes=64) for g in range(PASSES)
+        ]
+        wo_scales = [
+            keep.tile([P, N], U8, name="wo_scales%d" % g, align_bytes=64) for g in range(PASSES)
+        ]
+        for n in range(N_BLOCKS):
+            cols = slice(N_BLOCK * n, N_BLOCK * (n + 1))
+            for g in range(PASSES):
                 nc.vector.quantize_mx(
-                    out=codes[:, cols].bitcast(FP8X4),
-                    scales=scales[:, cols],
-                    in_=grouped[:, cols, :].rearrange("p c t -> p (c t)"),
+                    out=wo_codes[g][:, cols].bitcast(FP8X4),
+                    scales=wo_scales[g][:, cols],
+                    in_=wo_grouped[g][:, cols, :].rearrange("p c t -> p (c t)"),
                 )
-            wo_codes.append(codes)
-            wo_scales.append(scales)
 
         o_sb = [
             [keep.tile([P, N], F32, name="o_sb%d_%d" % (b, j)) for j in range(TILES)]
@@ -177,8 +180,8 @@ def tile_multiheadattn_pb_kernel(tc, h_attn, Wo, bo, x, gamma, beta, out):
                     out=o_sb[b][j][:], in0=bo_sb[b][:, j, :], in1=x_sb[b][:, j, :], op=ALU.add
                 )
 
-        def project(b):
-            for j in range(TILES):
+        def project(b, tiles):
+            for j in tiles:
                 for n in range(N_BLOCKS):
                     cols = slice(N_BLOCK * n, N_BLOCK * (n + 1))
                     acc = psum_acc.tile([P, N_BLOCK], F32, name="acc")
@@ -204,18 +207,18 @@ def tile_multiheadattn_pb_kernel(tc, h_attn, Wo, bo, x, gamma, beta, out):
                         accum_out=chunk_sums[b][:, chunk : chunk + 1],
                     )
 
-        def mean_over_all(sums):
-            row = scratch.tile([P, 1], F32, name="row")
-            nc.vector.reduce_sum(out=row[:], in_=sums[:], axis=AXIS.X)
-            mean = psum_stat.tile([P, 1], F32, name="mean")
-            nc.tensor.matmul(out=mean[:], lhsT=mean_w[:], rhs=row[:], start=True, stop=True)
-            return mean
+        def mean_over_all(result, sums, width, sign):
+            columns = psum_stat.tile([P, width], F32, name="columns")
+            nc.tensor.matmul(out=columns[:], lhsT=mean_w[:], rhs=sums[:], start=True, stop=True)
+            unread = scratch.tile([P, width], F32, name="unread")
+            nc.scalar.activation(
+                out=unread[:], in_=columns[:], func=ACT.Copy, scale=sign, accum_out=result[:]
+            )
 
         def find_mean(b):
-            mean = mean_over_all(chunk_sums[b])
-            nc.vector.tensor_scalar_mul(out=neg_mean[b][:], in0=mean[:], scalar1=-1.0)
+            mean_over_all(neg_mean[b], chunk_sums[b], TILES * N_BLOCKS, -1.0)
 
-        def find_rstd(b):
+        def sum_squares(b):
             for j in range(TILES):
                 squares = scratch.tile([P, N], BF16, name="squares")
                 nc.scalar.activation(
@@ -226,48 +229,51 @@ def tile_multiheadattn_pb_kernel(tc, h_attn, Wo, bo, x, gamma, beta, out):
                     scale=1.0,
                     accum_out=square_sums[b][:, j : j + 1],
                 )
-            var = mean_over_all(square_sums[b])
+
+        def find_rstd(b):
+            var = scratch.tile([P, 1], F32, name="var")
+            mean_over_all(var, square_sums[b], TILES, 1.0)
             std = scratch.tile([P, 1], F32, name="std")
             nc.scalar.activation(out=std[:], in_=var[:], func=ACT.Sqrt, bias=eps[:], scale=1.0)
             nc.vector.reciprocal(out=rstd[b][:], in_=std[:])
 
-        def centre_and_gain(b, j):
-            nc.vector.scalar_tensor_tensor(
-                out=o_sb[b][j][:],
-                in0=o_sb[b][j][:],
-                scalar=neg_mean[b][:],
-                in1=gamma_sb[:, j, :],
-                op0=ALU.add,
-                op1=ALU.mult,
-            )
+        def centre_and_gain(b):
+            for j in range(TILES):
+                nc.vector.scalar_tensor_tensor(
+                    out=o_sb[b][j][:],
+                    in0=o_sb[b][j][:],
+                    scalar=neg_mean[b][:],
+                    in1=gamma_sb[:, j, :],
+                    op0=ALU.add,
+                    op1=ALU.mult,
+                )
 
-        def scale_shift_store(b, j):
-            nc.vector.scalar_tensor_tensor(
-                out=o_sb[b][j][:],
-                in0=o_sb[b][j][:],
-                scalar=rstd[b][:],
-                in1=beta_sb[:, j, :],
-                op0=ALU.mult,
-                op1=ALU.add,
-            )
-            nc.sync.dma_start(out=out_view[b, :, j, :], in_=o_sb[b][j][:])
-
-        def normalise(b):
-            centre_and_gain(b, 0)
-            for j in range(1, TILES):
-                centre_and_gain(b, j)
-                scale_shift_store(b, j - 1)
-            scale_shift_store(b, TILES - 1)
+        def scale_shift_store(b):
+            for j in range(TILES):
+                nc.vector.scalar_tensor_tensor(
+                    out=o_sb[b][j][:],
+                    in0=o_sb[b][j][:],
+                    scalar=rstd[b][:],
+                    in1=beta_sb[:, j, :],
+                    op0=ALU.mult,
+                    op1=ALU.add,
+                )
+                nc.sync.dma_start(out=out_view[b, :, j, :], in_=o_sb[b][j][:])
 
         quantise_h(0)
+        quantise_h(1)
         add_bias_and_residual(nc.vector, 0)
         add_bias_and_residual(nc.gpsimd, 1)
-        project(0)
+        project(0, range(TILES))
+        project(1, range(1))
         find_mean(0)
-        quantise_h(1)
-        project(1)
-        find_rstd(0)
+        project(1, range(1, TILES))
+        sum_squares(0)
         find_mean(1)
-        normalise(0)
+        centre_and_gain(0)
+        find_rstd(0)
+        scale_shift_store(0)
+        sum_squares(1)
+        centre_and_gain(1)
         find_rstd(1)
-        normalise(1)
+        scale_shift_store(1)

@@ -25,6 +25,9 @@ HALVES = 2
 N_BLOCK = 512
 N_BLOCKS = N // N_BLOCK
 TILES = SEQ // P
+PAIR = 2
+PAIRS = BATCH * TILES // PAIR
+PAIRS_PER_BATCH = TILES // PAIR
 RUN = 4
 
 VECTOR_COLS = 672
@@ -38,8 +41,8 @@ def tile_multiheadattn_pb_kernel(tc, h_attn, Wo, bo, x, gamma, beta, out):
         const = ctx.enter_context(tc.tile_pool(name="const", bufs=1))
         keep = ctx.enter_context(tc.tile_pool(name="keep", bufs=1))
         scratch = ctx.enter_context(tc.tile_pool(name="scratch", bufs=4))
-        psum_t = ctx.enter_context(tc.psum_pool(name="psum_t", bufs=2))
-        psum_acc = ctx.enter_context(tc.psum_pool(name="psum_acc", bufs=4))
+        psum_t = ctx.enter_context(tc.psum_pool(name="psum_t", bufs=PAIR))
+        psum_acc = ctx.enter_context(tc.psum_pool(name="psum_acc", bufs=PAIR * N_BLOCKS))
         psum_stat = ctx.enter_context(tc.psum_pool(name="psum_stat", bufs=2))
         ctx.enter_context(tc.manual_schedule())
 
@@ -59,12 +62,9 @@ def tile_multiheadattn_pb_kernel(tc, h_attn, Wo, bo, x, gamma, beta, out):
         beta_view = beta.rearrange("(p j) n -> p j n", j=TILES)
         out_view = out.rearrange("b (p j) n -> b p j n", j=TILES)
 
-        def load_in_halves(dst, src):
-            half = TILES // 2
-            for first in (0, half):
-                nc.sync.dma_start(
-                    out=dst[:, first : first + half, :], in_=src[:, first : first + half, :]
-                )
+        def batch_and_tiles(pair):
+            first = PAIR * (pair % PAIRS_PER_BATCH)
+            return pair // PAIRS_PER_BATCH, range(first, first + PAIR)
 
         wo_raw = []
         for g in range(PASSES):
@@ -84,20 +84,18 @@ def tile_multiheadattn_pb_kernel(tc, h_attn, Wo, bo, x, gamma, beta, out):
         x_sb = [keep.tile([P, TILES, N], BF16, name="x_sb%d" % b) for b in range(BATCH)]
         gamma_sb = keep.tile([P, TILES, N], BF16)
         beta_sb = keep.tile([P, TILES, N], BF16)
-
-        def load_bias_and_residual(b):
-            half = TILES // 2
-            for first in (0, half):
-                tiles = slice(first, first + half)
-                nc.sync.dma_start(out=bo_sb[b][:, tiles, :], in_=bo_view[b, :, tiles, :])
-                nc.sync.dma_start(out=x_sb[b][:, tiles, :], in_=x_view[b, :, tiles, :])
-
-        load_in_halves(h_raw[0], h_view[0])
-        load_in_halves(h_raw[1], h_view[1])
-        load_bias_and_residual(0)
-        load_bias_and_residual(1)
-        load_in_halves(gamma_sb, gamma_view)
-        load_in_halves(beta_sb, beta_view)
+        for pair in range(PAIRS):
+            b, tiles = batch_and_tiles(pair)
+            both = slice(tiles[0], tiles[0] + PAIR)
+            nc.sync.dma_start(out=h_raw[b][:, both, :], in_=h_view[b, :, both, :])
+            nc.sync.dma_start(out=bo_sb[b][:, both, :], in_=bo_view[b, :, both, :])
+            nc.sync.dma_start(out=x_sb[b][:, both, :], in_=x_view[b, :, both, :])
+        for pair in range(PAIRS_PER_BATCH):
+            both = slice(PAIR * pair, PAIR * (pair + 1))
+            nc.sync.dma_start(out=gamma_sb[:, both, :], in_=gamma_view[:, both, :])
+        for pair in range(PAIRS_PER_BATCH):
+            both = slice(PAIR * pair, PAIR * (pair + 1))
+            nc.sync.dma_start(out=beta_sb[:, both, :], in_=beta_view[:, both, :])
 
         wo_grouped = []
         for g in range(PASSES):
@@ -151,8 +149,9 @@ def tile_multiheadattn_pb_kernel(tc, h_attn, Wo, bo, x, gamma, beta, out):
         neg_mean = [keep.tile([P, 1], F32, name="neg_mean%d" % b) for b in range(BATCH)]
         rstd = [keep.tile([P, 1], F32, name="rstd%d" % b) for b in range(BATCH)]
 
-        def quantise_h(b):
-            for j in range(TILES):
+        def quantise_h(pair):
+            b, tiles = batch_and_tiles(pair)
+            for j in tiles:
                 words = h_raw[b][:, j, :].bitcast(F32)
                 turned = psum_t.tile([P, PASSES, HALVES, P], F32, name="turned")
                 for g in range(PASSES):
@@ -174,13 +173,15 @@ def tile_multiheadattn_pb_kernel(tc, h_attn, Wo, bo, x, gamma, beta, out):
                     in_=grouped[:].rearrange("p g r t -> p (g r t)"),
                 )
 
-        def add_bias_and_residual(engine, b):
-            for j in range(TILES):
+        def add_bias_and_residual(pair):
+            b, tiles = batch_and_tiles(pair)
+            for engine, j in zip((nc.vector, nc.gpsimd), tiles):
                 engine.tensor_tensor(
                     out=o_sb[b][j][:], in0=bo_sb[b][:, j, :], in1=x_sb[b][:, j, :], op=ALU.add
                 )
 
-        def project(b, tiles):
+        def project(pair):
+            b, tiles = batch_and_tiles(pair)
             for j in tiles:
                 for n in range(N_BLOCKS):
                     cols = slice(N_BLOCK * n, N_BLOCK * (n + 1))
@@ -261,14 +262,17 @@ def tile_multiheadattn_pb_kernel(tc, h_attn, Wo, bo, x, gamma, beta, out):
                 nc.sync.dma_start(out=out_view[b, :, j, :], in_=o_sb[b][j][:])
 
         quantise_h(0)
-        quantise_h(1)
-        add_bias_and_residual(nc.vector, 0)
-        add_bias_and_residual(nc.gpsimd, 1)
-        project(0, range(TILES))
-        project(1, range(1))
-        find_mean(0)
-        project(1, range(1, TILES))
-        sum_squares(0)
+        add_bias_and_residual(0)
+        for pair in range(PAIRS):
+            if pair + 1 < PAIRS:
+                quantise_h(pair + 1)
+            project(pair)
+            if pair + 1 < PAIRS:
+                add_bias_and_residual(pair + 1)
+            if pair == PAIRS_PER_BATCH:
+                find_mean(0)
+                sum_squares(0)
+
         find_mean(1)
         centre_and_gain(0)
         find_rstd(0)

@@ -25,9 +25,6 @@ HALVES = 2
 N_BLOCK = 512
 N_BLOCKS = N // N_BLOCK
 TILES = SEQ // P
-PAIR = 2
-PAIRS = BATCH * TILES // PAIR
-PAIRS_PER_BATCH = TILES // PAIR
 RUN = 4
 
 VECTOR_COLS = 672
@@ -40,10 +37,10 @@ def tile_multiheadattn_pb_kernel(tc, h_attn, Wo, bo, x, gamma, beta, out):
     with ExitStack() as ctx:
         const = ctx.enter_context(tc.tile_pool(name="const", bufs=1))
         keep = ctx.enter_context(tc.tile_pool(name="keep", bufs=1))
-        scratch = ctx.enter_context(tc.tile_pool(name="scratch", bufs=4))
-        psum_t = ctx.enter_context(tc.psum_pool(name="psum_t", bufs=PAIR))
-        psum_acc = ctx.enter_context(tc.psum_pool(name="psum_acc", bufs=PAIR * N_BLOCKS))
-        psum_stat = ctx.enter_context(tc.psum_pool(name="psum_stat", bufs=2))
+        scratch = ctx.enter_context(tc.tile_pool(name="scratch", bufs=2))
+        psum_t = ctx.enter_context(tc.psum_pool(name="psum_t", bufs=3))
+        psum_acc = ctx.enter_context(tc.psum_pool(name="psum_acc", bufs=4))
+        psum_stat = ctx.enter_context(tc.psum_pool(name="psum_stat", bufs=1))
         ctx.enter_context(tc.manual_schedule())
 
         ident = const.tile([P, P], F32)
@@ -62,72 +59,48 @@ def tile_multiheadattn_pb_kernel(tc, h_attn, Wo, bo, x, gamma, beta, out):
         beta_view = beta.rearrange("(p j) n -> p j n", j=TILES)
         out_view = out.rearrange("b (p j) n -> b p j n", j=TILES)
 
-        def batch_and_tiles(pair):
-            first = PAIR * (pair % PAIRS_PER_BATCH)
-            return pair // PAIRS_PER_BATCH, range(first, first + PAIR)
-
-        wo_raw = []
-        for g in range(PASSES):
-            raw = keep.tile([P, PACK, N], BF16, name="wo_raw%d" % g)
-            for u in range(HALVES):
-                first = K_PASS * g + (K_PASS // HALVES) * u
-                nc.sync.dma_start(
-                    out=raw[:, 2 * u : 2 * u + 2, :],
-                    in_=Wo[first : first + K_PASS // HALVES, :].rearrange(
-                        "(q e) c -> q e c", e=2
-                    ),
-                )
-            wo_raw.append(raw)
-
+        wo_raw = [keep.tile([P, PACK, N], BF16, name="wo_raw%d" % g) for g in range(PASSES)]
         h_raw = [keep.tile([P, TILES, K], BF16, name="h_raw%d" % b) for b in range(BATCH)]
         bo_sb = [keep.tile([P, TILES, N], BF16, name="bo_sb%d" % b) for b in range(BATCH)]
         x_sb = [keep.tile([P, TILES, N], BF16, name="x_sb%d" % b) for b in range(BATCH)]
         gamma_sb = keep.tile([P, TILES, N], BF16)
         beta_sb = keep.tile([P, TILES, N], BF16)
-        for pair in range(PAIRS):
-            b, tiles = batch_and_tiles(pair)
-            both = slice(tiles[0], tiles[0] + PAIR)
-            nc.sync.dma_start(out=h_raw[b][:, both, :], in_=h_view[b, :, both, :])
-            nc.sync.dma_start(out=bo_sb[b][:, both, :], in_=bo_view[b, :, both, :])
-            nc.sync.dma_start(out=x_sb[b][:, both, :], in_=x_view[b, :, both, :])
-        for pair in range(PAIRS_PER_BATCH):
-            both = slice(PAIR * pair, PAIR * (pair + 1))
-            nc.sync.dma_start(out=gamma_sb[:, both, :], in_=gamma_view[:, both, :])
-        for pair in range(PAIRS_PER_BATCH):
-            both = slice(PAIR * pair, PAIR * (pair + 1))
-            nc.sync.dma_start(out=beta_sb[:, both, :], in_=beta_view[:, both, :])
 
-        wo_grouped = []
-        for g in range(PASSES):
-            grouped = keep.tile([P, N, PACK], BF16, name="wo_grouped%d" % g, align_bytes=64)
-            for copy, cols in (
-                (nc.vector.tensor_copy, slice(0, VECTOR_COLS)),
-                (nc.scalar.copy, slice(VECTOR_COLS, N)),
-            ):
-                copy(
-                    out=grouped[:, cols, :].rearrange("p (c i) t -> p c t i", i=RUN),
-                    in_=wo_raw[g][:, :, cols].rearrange("p t (c i) -> p c t i", i=RUN),
-                )
-            wo_grouped.append(grouped)
+        def load_in_halves(pairs):
+            half = TILES // 2
+            for first in (0, half):
+                for dst, src in pairs:
+                    nc.sync.dma_start(
+                        out=dst[:, first : first + half, :], in_=src[:, first : first + half, :]
+                    )
+
+        def load_wo():
+            for g in range(PASSES):
+                for u in range(HALVES):
+                    first = K_PASS * g + (K_PASS // HALVES) * u
+                    nc.sync.dma_start(
+                        out=wo_raw[g][:, 2 * u : 2 * u + 2, :],
+                        in_=Wo[first : first + K_PASS // HALVES, :].rearrange(
+                            "(q e) c -> q e c", e=2
+                        ),
+                    )
+
+        load_wo()
+        load_in_halves([(h_raw[0], h_view[0])])
+        load_in_halves([(h_raw[1], h_view[1])])
+        load_in_halves([(bo_sb[0], bo_view[0]), (x_sb[0], x_view[0])])
+        load_in_halves([(bo_sb[1], bo_view[1]), (x_sb[1], x_view[1])])
+        load_in_halves([(gamma_sb, gamma_view)])
+        load_in_halves([(beta_sb, beta_view)])
+
         wo_codes = [
             keep.tile([P, N], U32, name="wo_codes%d" % g, align_bytes=64) for g in range(PASSES)
         ]
         wo_scales = [
             keep.tile([P, N], U8, name="wo_scales%d" % g, align_bytes=64) for g in range(PASSES)
         ]
-        for n in range(N_BLOCKS):
-            cols = slice(N_BLOCK * n, N_BLOCK * (n + 1))
-            for g in range(PASSES):
-                nc.vector.quantize_mx(
-                    out=wo_codes[g][:, cols].bitcast(FP8X4),
-                    scales=wo_scales[g][:, cols],
-                    in_=wo_grouped[g][:, cols, :].rearrange("p c t -> p (c t)"),
-                )
-
-        o_sb = [
-            [keep.tile([P, N], F32, name="o_sb%d_%d" % (b, j)) for j in range(TILES)]
-            for b in range(BATCH)
-        ]
+        o_sb = [keep.tile([P, TILES, N], F32, name="o_sb%d" % b) for b in range(BATCH)]
+        out_sb = [keep.tile([P, TILES, N], F32, name="out_sb%d" % b) for b in range(BATCH)]
         h_codes = [
             [
                 keep.tile([P, PASSES * P], U32, name="h_codes%d_%d" % (b, j), align_bytes=64)
@@ -145,13 +118,34 @@ def tile_multiheadattn_pb_kernel(tc, h_attn, Wo, bo, x, gamma, beta, out):
         chunk_sums = [
             keep.tile([P, TILES * N_BLOCKS], F32, name="chunk_sums%d" % b) for b in range(BATCH)
         ]
-        square_sums = [keep.tile([P, TILES], F32, name="square_sums%d" % b) for b in range(BATCH)]
+        square_sums = [keep.tile([P, 1], F32, name="square_sums%d" % b) for b in range(BATCH)]
         neg_mean = [keep.tile([P, 1], F32, name="neg_mean%d" % b) for b in range(BATCH)]
         rstd = [keep.tile([P, 1], F32, name="rstd%d" % b) for b in range(BATCH)]
 
-        def quantise_h(pair):
-            b, tiles = batch_and_tiles(pair)
-            for j in tiles:
+        def quantise_wo():
+            wo_grouped = []
+            for g in range(PASSES):
+                grouped = keep.tile([P, N, PACK], BF16, name="wo_grouped%d" % g, align_bytes=64)
+                for copy, cols in (
+                    (nc.vector.tensor_copy, slice(0, VECTOR_COLS)),
+                    (nc.scalar.copy, slice(VECTOR_COLS, N)),
+                ):
+                    copy(
+                        out=grouped[:, cols, :].rearrange("p (c i) t -> p c t i", i=RUN),
+                        in_=wo_raw[g][:, :, cols].rearrange("p t (c i) -> p c t i", i=RUN),
+                    )
+                wo_grouped.append(grouped)
+            for n in range(N_BLOCKS):
+                cols = slice(N_BLOCK * n, N_BLOCK * (n + 1))
+                for g in range(PASSES):
+                    nc.vector.quantize_mx(
+                        out=wo_codes[g][:, cols].bitcast(FP8X4),
+                        scales=wo_scales[g][:, cols],
+                        in_=wo_grouped[g][:, cols, :].rearrange("p c t -> p (c t)"),
+                    )
+
+        def quantise_h(b):
+            for j in range(TILES):
                 words = h_raw[b][:, j, :].bitcast(F32)
                 turned = psum_t.tile([P, PASSES, HALVES, P], F32, name="turned")
                 for g in range(PASSES):
@@ -173,15 +167,15 @@ def tile_multiheadattn_pb_kernel(tc, h_attn, Wo, bo, x, gamma, beta, out):
                     in_=grouped[:].rearrange("p g r t -> p (g r t)"),
                 )
 
-        def add_bias_and_residual(pair):
-            b, tiles = batch_and_tiles(pair)
-            for engine, j in zip((nc.vector, nc.gpsimd), tiles):
-                engine.tensor_tensor(
-                    out=o_sb[b][j][:], in0=bo_sb[b][:, j, :], in1=x_sb[b][:, j, :], op=ALU.add
-                )
+        def add_bias_and_residual(engine, b, tiles):
+            engine.tensor_tensor(
+                out=o_sb[b][:, tiles, :],
+                in0=bo_sb[b][:, tiles, :],
+                in1=x_sb[b][:, tiles, :],
+                op=ALU.add,
+            )
 
-        def project(pair):
-            b, tiles = batch_and_tiles(pair)
+        def project(b, tiles):
             for j in tiles:
                 for n in range(N_BLOCKS):
                     cols = slice(N_BLOCK * n, N_BLOCK * (n + 1))
@@ -199,80 +193,86 @@ def tile_multiheadattn_pb_kernel(tc, h_attn, Wo, bo, x, gamma, beta, out):
                         )
                     chunk = N_BLOCKS * j + n
                     nc.vector.scalar_tensor_tensor(
-                        out=o_sb[b][j][:, cols],
+                        out=o_sb[b][:, j, cols],
                         in0=acc[:],
                         scalar=1.0,
-                        in1=o_sb[b][j][:, cols],
+                        in1=o_sb[b][:, j, cols],
                         op0=ALU.mult,
                         op1=ALU.add,
                         accum_out=chunk_sums[b][:, chunk : chunk + 1],
                     )
 
-        def mean_over_all(result, sums, width, sign):
-            columns = psum_stat.tile([P, width], F32, name="columns")
-            nc.tensor.matmul(out=columns[:], lhsT=mean_w[:], rhs=sums[:], start=True, stop=True)
-            unread = scratch.tile([P, width], F32, name="unread")
+        def find_mean(b):
+            chunks = TILES * N_BLOCKS
+            chunk_means = psum_stat.tile([P, chunks], F32, name="chunk_means", tag="stat")
+            nc.tensor.matmul(
+                out=chunk_means[:], lhsT=mean_w[:], rhs=chunk_sums[b][:], start=True, stop=True
+            )
+            unread = scratch.tile([P, chunks], F32, name="unread")
             nc.scalar.activation(
-                out=unread[:], in_=columns[:], func=ACT.Copy, scale=sign, accum_out=result[:]
+                out=unread[:],
+                in_=chunk_means[:],
+                func=ACT.Copy,
+                scale=-1.0,
+                accum_out=neg_mean[b][:],
             )
 
-        def find_mean(b):
-            mean_over_all(neg_mean[b], chunk_sums[b], TILES * N_BLOCKS, -1.0)
-
         def sum_squares(b):
-            for j in range(TILES):
-                squares = scratch.tile([P, N], BF16, name="squares")
-                nc.scalar.activation(
-                    out=squares[:],
-                    in_=o_sb[b][j][:],
-                    func=ACT.Square,
-                    bias=neg_mean[b][:],
-                    scale=1.0,
-                    accum_out=square_sums[b][:, j : j + 1],
-                )
+            squares = scratch.tile([P, TILES, N], BF16, name="squares")
+            nc.scalar.activation(
+                out=squares[:],
+                in_=o_sb[b][:],
+                func=ACT.Square,
+                bias=neg_mean[b][:],
+                scale=1.0,
+                accum_out=square_sums[b][:],
+            )
 
         def find_rstd(b):
-            var = scratch.tile([P, 1], F32, name="var")
-            mean_over_all(var, square_sums[b], TILES, 1.0)
+            var = psum_stat.tile([P, 1], F32, name="var", tag="stat")
+            nc.tensor.matmul(
+                out=var[:], lhsT=mean_w[:], rhs=square_sums[b][:], start=True, stop=True
+            )
             std = scratch.tile([P, 1], F32, name="std")
             nc.scalar.activation(out=std[:], in_=var[:], func=ACT.Sqrt, bias=eps[:], scale=1.0)
             nc.vector.reciprocal(out=rstd[b][:], in_=std[:])
 
         def centre_and_gain(b):
-            for j in range(TILES):
-                nc.vector.scalar_tensor_tensor(
-                    out=o_sb[b][j][:],
-                    in0=o_sb[b][j][:],
-                    scalar=neg_mean[b][:],
-                    in1=gamma_sb[:, j, :],
-                    op0=ALU.add,
-                    op1=ALU.mult,
-                )
+            nc.vector.scalar_tensor_tensor(
+                out=out_sb[b][:],
+                in0=o_sb[b][:],
+                scalar=neg_mean[b][:],
+                in1=gamma_sb[:],
+                op0=ALU.add,
+                op1=ALU.mult,
+            )
 
         def scale_shift_store(b):
             for j in range(TILES):
                 nc.vector.scalar_tensor_tensor(
-                    out=o_sb[b][j][:],
-                    in0=o_sb[b][j][:],
+                    out=out_sb[b][:, j, :],
+                    in0=out_sb[b][:, j, :],
                     scalar=rstd[b][:],
                     in1=beta_sb[:, j, :],
                     op0=ALU.mult,
                     op1=ALU.add,
                 )
-                nc.sync.dma_start(out=out_view[b, :, j, :], in_=o_sb[b][j][:])
+                nc.sync.dma_start(out=out_view[b, :, j, :], in_=out_sb[b][:, j, :])
 
+        quantise_wo()
         quantise_h(0)
-        add_bias_and_residual(0)
-        for pair in range(PAIRS):
-            if pair + 1 < PAIRS:
-                quantise_h(pair + 1)
-            project(pair)
-            if pair + 1 < PAIRS:
-                add_bias_and_residual(pair + 1)
-            if pair == PAIRS_PER_BATCH:
-                find_mean(0)
-                sum_squares(0)
+        add_bias_and_residual(nc.vector, 0, slice(0, TILES // 2))
+        quantise_h(1)
+        add_bias_and_residual(nc.vector, 0, slice(TILES // 2, TILES))
 
+        for j in range(TILES):
+            add_bias_and_residual(nc.gpsimd, 1, slice(j, j + 1))
+        project(0, range(TILES))
+        project(1, range(1))
+        find_mean(0)
+        project(1, range(1, TILES))
+
+        sum_squares(0)
         find_mean(1)
         centre_and_gain(0)
         find_rstd(0)

from contextlib import ExitStack

import concourse.mybir as mybir
from concourse.masks import make_identity

F32 = mybir.dt.float32
BF16 = mybir.dt.bfloat16
U32 = mybir.dt.uint32
U8 = mybir.dt.uint8
FP8X4 = mybir.dt.float8_e4m3fn_x4
ALU = mybir.AluOpType
ACT = mybir.ActivationFunctionType

P = 128
BATCH = 2
SEQ = 512
K = 1024
N = 1024
LN_EPS = 1e-5

PACK = 4
K_PASS = P * PACK
PASSES = K // K_PASS
HALVES = 2
N_BLOCK = 512
N_BLOCKS = N // N_BLOCK
TILES = SEQ // P
RUN = 4

VECTOR_COLS = 672

FLOPS = 2 * BATCH * SEQ * K * N


def tile_multiheadattn_pb_kernel(tc, h_attn, Wo, bo, x, gamma, beta, out):
    nc = tc.nc
    with ExitStack() as ctx:
        const = ctx.enter_context(tc.tile_pool(name="const", bufs=1))
        keep = ctx.enter_context(tc.tile_pool(name="keep", bufs=1))
        scratch = ctx.enter_context(tc.tile_pool(name="scratch", bufs=2))
        psum_t = ctx.enter_context(tc.psum_pool(name="psum_t", bufs=3))
        psum_acc = ctx.enter_context(tc.psum_pool(name="psum_acc", bufs=4))
        psum_stat = ctx.enter_context(tc.psum_pool(name="psum_stat", bufs=1))
        ctx.enter_context(tc.manual_schedule())

        ident = const.tile([P, P], F32)
        make_identity(nc, ident[:])
        mean_w = const.tile([P, P], F32)
        nc.vector.memset(mean_w[:], 1.0 / (SEQ * N))
        eps = const.tile([P, 1], F32)
        nc.vector.memset(eps[:], LN_EPS)
        warm = const.tile([P, 1], F32)
        nc.scalar.activation(out=warm[:], in_=eps[:], func=ACT.Sqrt)

        h_view = h_attn.rearrange("b (p j) k -> b p j k", j=TILES)
        bo_view = bo.rearrange("b (p j) n -> b p j n", j=TILES)
        x_view = x.rearrange("b (p j) n -> b p j n", j=TILES)
        gamma_view = gamma.rearrange("(p j) n -> p j n", j=TILES)
        beta_view = beta.rearrange("(p j) n -> p j n", j=TILES)
        out_view = out.rearrange("b (p j) n -> b p j n", j=TILES)

        wo_raw = [keep.tile([P, PACK, N], BF16, name="wo_raw%d" % g) for g in range(PASSES)]
        h_raw = [keep.tile([P, TILES, K], BF16, name="h_raw%d" % b) for b in range(BATCH)]
        bo_sb = [keep.tile([P, TILES, N], BF16, name="bo_sb%d" % b) for b in range(BATCH)]
        x_sb = [keep.tile([P, TILES, N], BF16, name="x_sb%d" % b) for b in range(BATCH)]
        gamma_sb = keep.tile([P, TILES, N], BF16)
        beta_sb = keep.tile([P, TILES, N], BF16)

        def load_in_halves(pairs):
            half = TILES // 2
            for first in (0, half):
                for dst, src in pairs:
                    nc.sync.dma_start(
                        out=dst[:, first : first + half, :], in_=src[:, first : first + half, :]
                    )

        def load_wo():
            for g in range(PASSES):
                for u in range(HALVES):
                    first = K_PASS * g + (K_PASS // HALVES) * u
                    nc.sync.dma_start(
                        out=wo_raw[g][:, 2 * u : 2 * u + 2, :],
                        in_=Wo[first : first + K_PASS // HALVES, :].rearrange(
                            "(q e) c -> q e c", e=2
                        ),
                    )

        load_wo()
        load_in_halves([(h_raw[0], h_view[0])])
        load_in_halves([(h_raw[1], h_view[1])])
        load_in_halves([(bo_sb[0], bo_view[0]), (x_sb[0], x_view[0])])
        load_in_halves([(bo_sb[1], bo_view[1]), (x_sb[1], x_view[1])])
        load_in_halves([(gamma_sb, gamma_view)])
        load_in_halves([(beta_sb, beta_view)])

        wo_codes = [
            keep.tile([P, N], U32, name="wo_codes%d" % g, align_bytes=64) for g in range(PASSES)
        ]
        wo_scales = [
            keep.tile([P, N], U8, name="wo_scales%d" % g, align_bytes=64) for g in range(PASSES)
        ]
        o_sb = [keep.tile([P, TILES, N], F32, name="o_sb%d" % b) for b in range(BATCH)]
        out_sb = [keep.tile([P, TILES, N], F32, name="out_sb%d" % b) for b in range(BATCH)]
        h_codes = [
            [
                keep.tile([P, PASSES * P], U32, name="h_codes%d_%d" % (b, j), align_bytes=64)
                for j in range(TILES)
            ]
            for b in range(BATCH)
        ]
        h_scales = [
            [
                keep.tile([P, PASSES * P], U8, name="h_scales%d_%d" % (b, j), align_bytes=64)
                for j in range(TILES)
            ]
            for b in range(BATCH)
        ]
        chunk_sums = [
            keep.tile([P, TILES * N_BLOCKS], F32, name="chunk_sums%d" % b) for b in range(BATCH)
        ]
        square_sums = [keep.tile([P, 1], F32, name="square_sums%d" % b) for b in range(BATCH)]
        neg_mean = [keep.tile([P, 1], F32, name="neg_mean%d" % b) for b in range(BATCH)]
        rstd = [keep.tile([P, 1], F32, name="rstd%d" % b) for b in range(BATCH)]

        def quantise_wo():
            wo_grouped = []
            for g in range(PASSES):
                grouped = keep.tile([P, N, PACK], BF16, name="wo_grouped%d" % g, align_bytes=64)
                for copy, cols in (
                    (nc.vector.tensor_copy, slice(0, VECTOR_COLS)),
                    (nc.scalar.copy, slice(VECTOR_COLS, N)),
                ):
                    copy(
                        out=grouped[:, cols, :].rearrange("p (c i) t -> p c t i", i=RUN),
                        in_=wo_raw[g][:, :, cols].rearrange("p t (c i) -> p c t i", i=RUN),
                    )
                wo_grouped.append(grouped)
            for n in range(N_BLOCKS):
                cols = slice(N_BLOCK * n, N_BLOCK * (n + 1))
                for g in range(PASSES):
                    nc.vector.quantize_mx(
                        out=wo_codes[g][:, cols].bitcast(FP8X4),
                        scales=wo_scales[g][:, cols],
                        in_=wo_grouped[g][:, cols, :].rearrange("p c t -> p (c t)"),
                    )

        def quantise_h(b):
            for j in range(TILES):
                words = h_raw[b][:, j, :].bitcast(F32)
                turned = psum_t.tile([P, PASSES, HALVES, P], F32, name="turned")
                for g in range(PASSES):
                    for u in range(HALVES):
                        first = P * (HALVES * g + u)
                        nc.tensor.transpose(
                            turned[:, g, u, :], words[:, first : first + P], ident[:]
                        )
                grouped = keep.tile(
                    [P, PASSES, P, PACK], BF16, name="h_grouped%d_%d" % (b, j), align_bytes=64
                )
                nc.scalar.copy(
                    out=grouped[:].bitcast(F32),
                    in_=turned[:].rearrange("p g u r -> p g r u"),
                )
                nc.vector.quantize_mx(
                    out=h_codes[b][j][:].bitcast(FP8X4),
                    scales=h_scales[b][j][:],
                    in_=grouped[:].rearrange("p g r t -> p (g r t)"),
                )

        def add_bias_and_residual(engine, b, tiles):
            engine.tensor_tensor(
                out=o_sb[b][:, tiles, :],
                in0=bo_sb[b][:, tiles, :],
                in1=x_sb[b][:, tiles, :],
                op=ALU.add,
            )

        def project(b, tiles):
            for j in tiles:
                for n in range(N_BLOCKS):
                    cols = slice(N_BLOCK * n, N_BLOCK * (n + 1))
                    acc = psum_acc.tile([P, N_BLOCK], F32, name="acc")
                    for g in range(PASSES):
                        tokens = slice(P * g, P * (g + 1))
                        nc.tensor.matmul_mx(
                            out=acc[:],
                            lhsT=h_codes[b][j][:, tokens].bitcast(FP8X4),
                            lhsT_scale=h_scales[b][j][:, tokens],
                            rhs=wo_codes[g][:, cols].bitcast(FP8X4),
                            rhs_scale=wo_scales[g][:, cols],
                            start=(g == 0),
                            stop=(g == PASSES - 1),
                        )
                    chunk = N_BLOCKS * j + n
                    nc.vector.scalar_tensor_tensor(
                        out=o_sb[b][:, j, cols],
                        in0=acc[:],
                        scalar=1.0,
                        in1=o_sb[b][:, j, cols],
                        op0=ALU.mult,
                        op1=ALU.add,
                        accum_out=chunk_sums[b][:, chunk : chunk + 1],
                    )

        def find_mean(b):
            chunks = TILES * N_BLOCKS
            chunk_means = psum_stat.tile([P, chunks], F32, name="chunk_means", tag="stat")
            nc.tensor.matmul(
                out=chunk_means[:], lhsT=mean_w[:], rhs=chunk_sums[b][:], start=True, stop=True
            )
            unread = scratch.tile([P, chunks], F32, name="unread")
            nc.scalar.activation(
                out=unread[:],
                in_=chunk_means[:],
                func=ACT.Copy,
                scale=-1.0,
                accum_out=neg_mean[b][:],
            )

        def sum_squares(b):
            squares = scratch.tile([P, TILES, N], BF16, name="squares")
            nc.scalar.activation(
                out=squares[:],
                in_=o_sb[b][:],
                func=ACT.Square,
                bias=neg_mean[b][:],
                scale=1.0,
                accum_out=square_sums[b][:],
            )

        def find_rstd(b):
            var = psum_stat.tile([P, 1], F32, name="var", tag="stat")
            nc.tensor.matmul(
                out=var[:], lhsT=mean_w[:], rhs=square_sums[b][:], start=True, stop=True
            )
            std = scratch.tile([P, 1], F32, name="std")
            nc.scalar.activation(out=std[:], in_=var[:], func=ACT.Sqrt, bias=eps[:], scale=1.0)
            nc.vector.reciprocal(out=rstd[b][:], in_=std[:])

        def centre_and_gain(b):
            nc.vector.scalar_tensor_tensor(
                out=out_sb[b][:],
                in0=o_sb[b][:],
                scalar=neg_mean[b][:],
                in1=gamma_sb[:],
                op0=ALU.add,
                op1=ALU.mult,
            )

        def scale_shift_store(b):
            for j in range(TILES):
                nc.vector.scalar_tensor_tensor(
                    out=out_sb[b][:, j, :],
                    in0=out_sb[b][:, j, :],
                    scalar=rstd[b][:],
                    in1=beta_sb[:, j, :],
                    op0=ALU.mult,
                    op1=ALU.add,
                )
                nc.sync.dma_start(out=out_view[b, :, j, :], in_=out_sb[b][:, j, :])

        quantise_wo()
        quantise_h(0)
        add_bias_and_residual(nc.vector, 0, slice(0, TILES // 2))
        quantise_h(1)
        add_bias_and_residual(nc.vector, 0, slice(TILES // 2, TILES))

        for j in range(TILES):
            add_bias_and_residual(nc.gpsimd, 1, slice(j, j + 1))
        project(0, range(TILES))
        project(1, range(1))
        find_mean(0)
        project(1, range(1, TILES))

        sum_squares(0)
        find_mean(1)
        centre_and_gain(0)
        find_rstd(0)
        scale_shift_store(0)
        sum_squares(1)
        centre_and_gain(1)
        find_rstd(1)
        scale_shift_store(1)
